import numpy as np
import ml_dtypes

BF16 = ml_dtypes.bfloat16


def bf(x):
    return np.asarray(x, np.float32).astype(BF16)


def f32(x):
    return np.asarray(x, np.float32)


def f64(x):
    return np.asarray(x).astype(np.float64)


def striped(idx):
    return np.tile(idx.reshape(-1, 16).T, (8, 1))


C, S, F, R, N = 256, 1152, 128, 3, 3456


def setup_inputs():
    return {"x": f32(0.25 * np.random.standard_normal((C, S))), "w_hit": f32(np.random.standard_normal((S, F))), "w_miss": f32(np.random.standard_normal((S, F))), "gamma": f32(-0.5 - 0.1 * np.random.rand(1)), "offs": striped(np.concatenate([np.random.permutation(S) for _ in range(R)]))}


def reference(x, w_hit, w_miss, gamma, offs):
    idx = offs[:16].T.reshape(-1)
    xx = f64(x)
    sel = 0.5 * (1.0 + np.sign(xx))
    mag = np.abs(xx)
    hit = mag.copy()
    for r in range(R):
        hit = sel[:, idx[r * S:(r + 1) * S]] * hit
    miss = mag - hit
    return np.abs(f64(gamma))[0] * (hit @ np.sign(f64(w_hit)) + miss @ np.sign(f64(w_miss)))

@@ -1,0 +1,100 @@
+import concourse.mybir as mybir
+from concourse.masks import make_identity
+
+F32 = mybir.dt.float32
+BF16 = mybir.dt.bfloat16
+U16 = mybir.dt.uint16
+ACT = mybir.ActivationFunctionType
+ALU = mybir.AluOpType
+
+P = 128
+C, S, F, R = 256, 1152, 128, 3
+BLOCKS = C // P
+PIECE = 384
+PIECES = S // PIECE
+TILES = PIECE // P
+RUN_COLS = S // 16
+PIECE_COLS = PIECE // 16
+
+FLOPS = 2 * 2 * C * S * F
+
+
+def tile_binary_conv_kernel(tc, x, w_hit, w_miss, gamma, offs, out):
+    nc = tc.nc
+    with (
+        tc.tile_pool(name="held", bufs=1) as held,
+        tc.tile_pool(name="block", bufs=BLOCKS) as block,
+        tc.tile_pool(name="work", bufs=3) as work,
+        tc.psum_pool(name="flip", bufs=2) as flip,
+        tc.psum_pool(name="sums", bufs=BLOCKS) as sums,
+    ):
+        offsets = held.tile([P, R * RUN_COLS], U16, name="offsets")
+        nc.sync.dma_start(offsets[:], offs)
+        x_blocks = []
+        for b, queue in zip(range(BLOCKS), (nc.scalar, nc.gpsimd)):
+            x_sb = block.tile([P, S], F32, name="x_sb")
+            queue.dma_start(x_sb[:], x[b * P : (b + 1) * P, :])
+            x_blocks.append(x_sb)
+        gamma_sb = held.tile([P, 1], F32, name="gamma_sb")
+        nc.sync.dma_start(gamma_sb[:], gamma.partition_broadcast(P))
+        w_raw = {}
+        for name, w in (("hit", w_hit), ("miss", w_miss)):
+            w_raw[name] = held.tile([P, S // P, F], F32, name="w_raw_" + name)
+            nc.sync.dma_start(w_raw[name][:], w.rearrange("(k p) f -> p k f", p=P))
+
+        identity = held.tile([P, P], F32, name="identity")
+        make_identity(nc, identity[:])
+
+        sel_blocks, mag_blocks = [], []
+        for b in range(BLOCKS):
+            sgn = block.tile([P, S], F32, name="sgn")
+            nc.scalar.activation(sgn[:], x_blocks[b][:], ACT.Sign)
+            sel = block.tile([P, S], F32, name="sel")
+            halver = nc.vector if b == 0 else nc.gpsimd
+            halver.tensor_scalar(sel[:], sgn[:], 0.5, 0.5, ALU.mult, ALU.add)
+            mag = block.tile([P, S], F32, name="mag")
+            nc.scalar.activation(mag[:], x_blocks[b][:], ACT.Abs)
+            sel_blocks.append(sel)
+            mag_blocks.append(mag)
+
+        w_sign = {}
+        for name in ("hit", "miss"):
+            w_sign[name] = held.tile([P, S // P, F], BF16, name="w_sign_" + name)
+            nc.scalar.activation(w_sign[name][:], w_raw[name][:], ACT.Sign)
+        gamma_abs = held.tile([P, 1], F32, name="gamma_abs")
+        nc.scalar.activation(gamma_abs[:], gamma_sb[:], ACT.Abs)
+
+        for b in range(BLOCKS):
+            sel, mag = sel_blocks[b], mag_blocks[b]
+            total = sums.tile([P, F], F32, name="total")
+            for i in range(PIECES):
+                taps = slice(i * PIECE, (i + 1) * PIECE)
+                product = mag[:, taps]
+                for r in range(R):
+                    first = r * RUN_COLS + i * PIECE_COLS
+                    picked = sel[:].indirect(offsets[:, first : first + PIECE_COLS])
+                    longer = work.tile([P, PIECE], F32, name="product" + str(r))
+                    nc.vector.tensor_tensor(longer[:], picked, product, ALU.mult)
+                    product = longer[:]
+                hit = product
+                miss = work.tile([P, PIECE], F32, name="miss")
+                nc.gpsimd.tensor_tensor(miss[:], mag[:, taps], hit, ALU.subtract)
+
+                flipped = {}
+                for name, rows in (("hit", hit), ("miss", miss[:])):
+                    turned = flip.tile([P, PIECE], F32, name="turned_" + name)
+                    for t in range(TILES):
+                        cols = slice(t * P, (t + 1) * P)
+                        nc.tensor.transpose(turned[:, cols], rows[:, cols], identity[:])
+                    flipped[name] = work.tile([P, PIECE], BF16, name="flipped_" + name)
+                    nc.scalar.copy(flipped[name][:], turned[:])
+                for t in range(TILES):
+                    k = i * TILES + t
+                    cols = slice(t * P, (t + 1) * P)
+                    nc.tensor.matmul(total[:], flipped["hit"][:, cols], w_sign["hit"][:, k, :],
+                                     start=(k == 0), stop=False)
+                    nc.tensor.matmul(total[:], flipped["miss"][:, cols], w_sign["miss"][:, k, :],
+                                     start=False, stop=(k == S // P - 1))
+            scaled = work.tile([P, F], F32, name="scaled")
+            nc.scalar.mul(scaled[:], total[:], gamma_abs[:, 0:1])
+            nc.sync.dma_start(out[b * P : (b + 1) * P, :], scaled[:])

@@ -50,8 +50,7 @@ def tile_binary_conv_kernel(tc, x, w_hit, w_miss, gamma, offs, out):
             sgn = block.tile([P, S], F32, name="sgn")
             nc.scalar.activation(sgn[:], x_blocks[b][:], ACT.Sign)
             sel = block.tile([P, S], F32, name="sel")
-            halver = nc.vector if b == 0 else nc.gpsimd
-            halver.tensor_scalar(sel[:], sgn[:], 0.5, 0.5, ALU.mult, ALU.add)
+            nc.vector.tensor_scalar(sel[:], sgn[:], 0.5, 0.5, ALU.mult, ALU.add)
             mag = block.tile([P, S], F32, name="mag")
             nc.scalar.activation(mag[:], x_blocks[b][:], ACT.Abs)
             sel_blocks.append(sel)
@@ -78,7 +77,7 @@ def tile_binary_conv_kernel(tc, x, w_hit, w_miss, gamma, offs, out):
                     product = longer[:]
                 hit = product
                 miss = work.tile([P, PIECE], F32, name="miss")
-                nc.gpsimd.tensor_tensor(miss[:], mag[:, taps], hit, ALU.subtract)
+                nc.vector.tensor_tensor(miss[:], mag[:, taps], hit, ALU.subtract)
 
                 flipped = {}
                 for name, rows in (("hit", hit), ("miss", miss[:])):

@@ -31,7 +31,7 @@ def tile_binary_conv_kernel(tc, x, w_hit, w_miss, gamma, offs, out):
         offsets = held.tile([P, R * RUN_COLS], U16, name="offsets")
         nc.sync.dma_start(offsets[:], offs)
         x_blocks = []
-        for b, queue in zip(range(BLOCKS), (nc.scalar, nc.gpsimd)):
+        for b, queue in zip(range(BLOCKS), (nc.scalar, nc.sync)):
             x_sb = block.tile([P, S], F32, name="x_sb")
             queue.dma_start(x_sb[:], x[b * P : (b + 1) * P, :])
             x_blocks.append(x_sb)
@@ -40,12 +40,12 @@ def tile_binary_conv_kernel(tc, x, w_hit, w_miss, gamma, offs, out):
         w_raw = {}
         for name, w in (("hit", w_hit), ("miss", w_miss)):
             w_raw[name] = held.tile([P, S // P, F], F32, name="w_raw_" + name)
-            nc.sync.dma_start(w_raw[name][:], w.rearrange("(k p) f -> p k f", p=P))
+            nc.scalar.dma_start(w_raw[name][:], w.rearrange("(k p) f -> p k f", p=P))
 
         identity = held.tile([P, P], F32, name="identity")
         make_identity(nc, identity[:])
 
-        sel_blocks, mag_blocks = [], []
+        sel_blocks, mag_blocks, minus_mag_blocks = [], [], []
         for b in range(BLOCKS):
             sgn = block.tile([P, S], F32, name="sgn")
             nc.scalar.activation(sgn[:], x_blocks[b][:], ACT.Sign)
@@ -53,8 +53,11 @@ def tile_binary_conv_kernel(tc, x, w_hit, w_miss, gamma, offs, out):
             nc.vector.tensor_scalar(sel[:], sgn[:], 0.5, 0.5, ALU.mult, ALU.add)
             mag = block.tile([P, S], F32, name="mag")
             nc.scalar.activation(mag[:], x_blocks[b][:], ACT.Abs)
+            minus_mag = block.tile([P, S], F32, name="minus_mag")
+            nc.scalar.mul(minus_mag[:], mag[:], -1.0)
             sel_blocks.append(sel)
             mag_blocks.append(mag)
+            minus_mag_blocks.append(minus_mag)
 
         w_sign = {}
         for name in ("hit", "miss"):
@@ -64,7 +67,7 @@ def tile_binary_conv_kernel(tc, x, w_hit, w_miss, gamma, offs, out):
         nc.scalar.activation(gamma_abs[:], gamma_sb[:], ACT.Abs)
 
         for b in range(BLOCKS):
-            sel, mag = sel_blocks[b], mag_blocks[b]
+            sel, mag, minus_mag = sel_blocks[b], mag_blocks[b], minus_mag_blocks[b]
             total = sums.tile([P, F], F32, name="total")
             for i in range(PIECES):
                 taps = slice(i * PIECE, (i + 1) * PIECE)
@@ -76,23 +79,27 @@ def tile_binary_conv_kernel(tc, x, w_hit, w_miss, gamma, offs, out):
                     nc.vector.tensor_tensor(longer[:], picked, product, ALU.mult)
                     product = longer[:]
                 hit = product
-                miss = work.tile([P, PIECE], F32, name="miss")
-                nc.vector.tensor_tensor(miss[:], mag[:, taps], hit, ALU.subtract)
 
-                flipped = {}
-                for name, rows in (("hit", hit), ("miss", miss[:])):
-                    turned = flip.tile([P, PIECE], F32, name="turned_" + name)
-                    for t in range(TILES):
-                        cols = slice(t * P, (t + 1) * P)
-                        nc.tensor.transpose(turned[:, cols], rows[:, cols], identity[:])
-                    flipped[name] = work.tile([P, PIECE], BF16, name="flipped_" + name)
-                    nc.scalar.copy(flipped[name][:], turned[:])
+                turned_hit = flip.tile([P, PIECE], F32, name="turned_hit")
+                turned_minus_miss = flip.tile([P, PIECE], F32, name="turned_minus_miss")
+                for t in range(TILES):
+                    cols = slice(t * P, (t + 1) * P)
+                    k = i * TILES + t
+                    nc.tensor.transpose(turned_hit[:, cols], hit[:, cols], identity[:])
+                    nc.tensor.matmul(turned_minus_miss[:, cols], minus_mag[:, k * P : (k + 1) * P],
+                                     identity[:], is_transpose=True, start=True, stop=False)
+                    nc.tensor.matmul(turned_minus_miss[:, cols], hit[:, cols],
+                                     identity[:], is_transpose=True, start=False, stop=True)
+                flipped_hit = work.tile([P, PIECE], BF16, name="flipped_hit")
+                nc.scalar.copy(flipped_hit[:], turned_hit[:])
+                flipped_miss = work.tile([P, PIECE], BF16, name="flipped_miss")
+                nc.scalar.mul(flipped_miss[:], turned_minus_miss[:], -1.0)
                 for t in range(TILES):
                     k = i * TILES + t
                     cols = slice(t * P, (t + 1) * P)
-                    nc.tensor.matmul(total[:], flipped["hit"][:, cols], w_sign["hit"][:, k, :],
+                    nc.tensor.matmul(total[:], flipped_hit[:, cols], w_sign["hit"][:, k, :],
                                      start=(k == 0), stop=False)
-                    nc.tensor.matmul(total[:], flipped["miss"][:, cols], w_sign["miss"][:, k, :],
+                    nc.tensor.matmul(total[:], flipped_miss[:, cols], w_sign["miss"][:, k, :],
                                      start=False, stop=(k == S // P - 1))
             scaled = work.tile([P, F], F32, name="scaled")
             nc.scalar.mul(scaled[:], total[:], gamma_abs[:, 0:1])

@@ -69,16 +69,17 @@ def tile_binary_conv_kernel(tc, x, w_hit, w_miss, gamma, offs, out):
         for b in range(BLOCKS):
             sel, mag, minus_mag = sel_blocks[b], mag_blocks[b], minus_mag_blocks[b]
             total = sums.tile([P, F], F32, name="total")
-            for i in range(PIECES):
-                taps = slice(i * PIECE, (i + 1) * PIECE)
-                product = mag[:, taps]
-                for r in range(R):
+            product = mag
+            for r in range(R):
+                longer = block.tile([P, S], F32, name="product" + str(r))
+                for i in range(PIECES):
+                    taps = slice(i * PIECE, (i + 1) * PIECE)
                     first = r * RUN_COLS + i * PIECE_COLS
                     picked = sel[:].indirect(offsets[:, first : first + PIECE_COLS])
-                    longer = work.tile([P, PIECE], F32, name="product" + str(r))
-                    nc.vector.tensor_tensor(longer[:], picked, product, ALU.mult)
-                    product = longer[:]
-                hit = product
+                    nc.vector.tensor_tensor(longer[:, taps], picked, product[:, taps], ALU.mult)
+                product = longer
+            for i in range(PIECES):
+                hit = product[:, i * PIECE : (i + 1) * PIECE]
 
                 turned_hit = flip.tile([P, PIECE], F32, name="turned_hit")
                 turned_minus_miss = flip.tile([P, PIECE], F32, name="turned_minus_miss")

@@ -10,11 +10,12 @@ ALU = mybir.AluOpType
 P = 128
 C, S, F, R = 256, 1152, 128, 3
 BLOCKS = C // P
-PIECE = 384
-PIECES = S // PIECE
-TILES = PIECE // P
+K_TILES = S // P
 RUN_COLS = S // 16
-PIECE_COLS = PIECE // 16
+PIECES = ((512, 640), (640, 256, 128, 128))
+WIDEST = max(max(widths) for widths in PIECES)
+UNIT = 256
+X0_CUTS = 3
 
 FLOPS = 2 * 2 * C * S * F
 
@@ -25,83 +26,87 @@ def tile_binary_conv_kernel(tc, x, w_hit, w_miss, gamma, offs, out):
         tc.tile_pool(name="held", bufs=1) as held,
         tc.tile_pool(name="block", bufs=BLOCKS) as block,
         tc.tile_pool(name="work", bufs=3) as work,
-        tc.psum_pool(name="flip", bufs=2) as flip,
+        tc.psum_pool(name="flip", bufs=4) as flip,
         tc.psum_pool(name="sums", bufs=BLOCKS) as sums,
     ):
         offsets = held.tile([P, R * RUN_COLS], U16, name="offsets")
         nc.sync.dma_start(offsets[:], offs)
-        x_blocks = []
-        for b, queue in zip(range(BLOCKS), (nc.scalar, nc.sync)):
-            x_sb = block.tile([P, S], F32, name="x_sb")
-            queue.dma_start(x_sb[:], x[b * P : (b + 1) * P, :])
-            x_blocks.append(x_sb)
-        gamma_sb = held.tile([P, 1], F32, name="gamma_sb")
-        nc.sync.dma_start(gamma_sb[:], gamma.partition_broadcast(P))
+        cuts = {0: X0_CUTS, 1: 1}
+        x_blocks = [block.tile([P, S], F32, name="x_sb") for b in range(BLOCKS)]
+        for j in range(X0_CUTS):
+            cols = slice(j * (S // X0_CUTS), (j + 1) * (S // X0_CUTS))
+            queue = nc.scalar if j % 2 == 0 else nc.sync
+            queue.dma_start(x_blocks[0][:, cols], x[0:P, cols])
         w_raw = {}
-        for name, w in (("hit", w_hit), ("miss", w_miss)):
-            w_raw[name] = held.tile([P, S // P, F], F32, name="w_raw_" + name)
-            nc.scalar.dma_start(w_raw[name][:], w.rearrange("(k p) f -> p k f", p=P))
+        for name, w, queue in (("hit", w_hit, nc.sync), ("miss", w_miss, nc.scalar)):
+            w_raw[name] = held.tile([P, K_TILES, F], F32, name="w_raw_" + name)
+            queue.dma_start(w_raw[name][:], w.rearrange("(k p) f -> p k f", p=P))
+        nc.sync.dma_start(x_blocks[1][:], x[P : 2 * P, :])
+        gamma_sb = held.tile([P, 1], F32, name="gamma_sb")
+        nc.scalar.dma_start(gamma_sb[:], gamma.partition_broadcast(P))
 
         identity = held.tile([P, P], F32, name="identity")
         make_identity(nc, identity[:])
 
-        sel_blocks, mag_blocks, minus_mag_blocks = [], [], []
-        for b in range(BLOCKS):
-            sgn = block.tile([P, S], F32, name="sgn")
-            nc.scalar.activation(sgn[:], x_blocks[b][:], ACT.Sign)
-            sel = block.tile([P, S], F32, name="sel")
-            nc.vector.tensor_scalar(sel[:], sgn[:], 0.5, 0.5, ALU.mult, ALU.add)
-            mag = block.tile([P, S], F32, name="mag")
-            nc.scalar.activation(mag[:], x_blocks[b][:], ACT.Abs)
-            minus_mag = block.tile([P, S], F32, name="minus_mag")
-            nc.scalar.mul(minus_mag[:], mag[:], -1.0)
-            sel_blocks.append(sel)
-            mag_blocks.append(mag)
-            minus_mag_blocks.append(minus_mag)
-
+        sel_blocks, minus_x_blocks = [], []
         w_sign = {}
-        for name in ("hit", "miss"):
-            w_sign[name] = held.tile([P, S // P, F], BF16, name="w_sign_" + name)
-            nc.scalar.activation(w_sign[name][:], w_raw[name][:], ACT.Sign)
-        gamma_abs = held.tile([P, 1], F32, name="gamma_abs")
-        nc.scalar.activation(gamma_abs[:], gamma_sb[:], ACT.Abs)
-
         for b in range(BLOCKS):
-            sel, mag, minus_mag = sel_blocks[b], mag_blocks[b], minus_mag_blocks[b]
-            total = sums.tile([P, F], F32, name="total")
-            product = mag
-            for r in range(R):
-                longer = block.tile([P, S], F32, name="product" + str(r))
-                for i in range(PIECES):
-                    taps = slice(i * PIECE, (i + 1) * PIECE)
-                    first = r * RUN_COLS + i * PIECE_COLS
-                    picked = sel[:].indirect(offsets[:, first : first + PIECE_COLS])
-                    nc.vector.tensor_tensor(longer[:, taps], picked, product[:, taps], ALU.mult)
-                product = longer
-            for i in range(PIECES):
-                hit = product[:, i * PIECE : (i + 1) * PIECE]
+            x_sb = x_blocks[b]
+            sgn = block.tile([P, S], F32, name="sgn")
+            sel = block.tile([P, S], F32, name="sel")
+            for j in range(cuts[b]):
+                cols = slice(j * (S // cuts[b]), (j + 1) * (S // cuts[b]))
+                nc.scalar.activation(sgn[:, cols], x_sb[:, cols], ACT.Sign)
+                if b == 0:
+                    nc.vector.tensor_scalar(sel[:, cols], sgn[:, cols], 0.5, 0.5, ALU.mult, ALU.add)
+                else:
+                    nc.scalar.activation(sel[:, cols], sgn[:, cols], ACT.Copy, bias=0.5, scale=0.5)
+            minus_x = block.tile([P, S], F32, name="minus_x")
+            nc.scalar.mul(minus_x[:], x_sb[:], -1.0)
+            sel_blocks.append(sel)
+            minus_x_blocks.append(minus_x)
+            if b == 0:
+                for name in ("hit", "miss"):
+                    w_sign[name] = held.tile([P, K_TILES, F], BF16, name="w_sign_" + name)
+                    nc.scalar.activation(w_sign[name][:], w_raw[name][:], ACT.Sign)
+                gamma_abs = held.tile([P, 1], F32, name="gamma_abs")
+                nc.scalar.activation(gamma_abs[:], gamma_sb[:], ACT.Abs)
 
-                turned_hit = flip.tile([P, PIECE], F32, name="turned_hit")
-                turned_minus_miss = flip.tile([P, PIECE], F32, name="turned_minus_miss")
-                for t in range(TILES):
-                    cols = slice(t * P, (t + 1) * P)
-                    k = i * TILES + t
-                    nc.tensor.transpose(turned_hit[:, cols], hit[:, cols], identity[:])
-                    nc.tensor.matmul(turned_minus_miss[:, cols], minus_mag[:, k * P : (k + 1) * P],
-                                     identity[:], is_transpose=True, start=True, stop=False)
-                    nc.tensor.matmul(turned_minus_miss[:, cols], hit[:, cols],
-                                     identity[:], is_transpose=True, start=False, stop=True)
-                flipped_hit = work.tile([P, PIECE], BF16, name="flipped_hit")
-                nc.scalar.copy(flipped_hit[:], turned_hit[:])
-                flipped_miss = work.tile([P, PIECE], BF16, name="flipped_miss")
-                nc.scalar.mul(flipped_miss[:], turned_minus_miss[:], -1.0)
-                for t in range(TILES):
-                    k = i * TILES + t
-                    cols = slice(t * P, (t + 1) * P)
-                    nc.tensor.matmul(total[:], flipped_hit[:, cols], w_sign["hit"][:, k, :],
-                                     start=(k == 0), stop=False)
-                    nc.tensor.matmul(total[:], flipped_miss[:, cols], w_sign["miss"][:, k, :],
-                                     start=False, stop=(k == S // P - 1))
+        HIT, MISS = 0, 1
+        for b in range(BLOCKS):
+            x_sb, sel, minus_x = x_blocks[b], sel_blocks[b], minus_x_blocks[b]
+            total = sums.tile([P, F], F32, name="total")
+            piece_tap = 0
+            for width in PIECES[b]:
+                signed = x_sb[:, piece_tap : piece_tap + width]
+                for r in range(R):
+                    first = r * RUN_COLS + piece_tap // 16
+                    picked = sel[:].indirect(offsets[:, first : first + width // 16])
+                    longer = work.tile([P, WIDEST], F32, name="product" + str(r))
+                    nc.vector.tensor_tensor(longer[:, :width], picked, signed, ALU.mult)
+                    signed = longer[:, :width]
+
+                for unit_col in range(0, width, UNIT):
+                    unit_width = min(UNIT, width - unit_col)
+                    unit_tap = piece_tap + unit_col
+                    turned = flip.tile([P, 2, unit_width], F32, name="turned")
+                    for col in range(0, unit_width, P):
+                        rows = signed[:, unit_col + col : unit_col + col + P]
+                        nc.tensor.matmul(turned[:, MISS, col : col + P],
+                                         minus_x[:, unit_tap + col : unit_tap + col + P], identity[:],
+                                         is_transpose=True, start=True, stop=False)
+                        nc.tensor.matmul(turned[:, MISS, col : col + P], rows, identity[:],
+                                         is_transpose=True, start=False, stop=True)
+                        nc.tensor.transpose(turned[:, HIT, col : col + P], rows, identity[:])
+                    flipped = work.tile([P, 2, unit_width], BF16, name="flipped")
+                    nc.scalar.activation(flipped[:], turned[:], ACT.Abs)
+                    for col in range(0, unit_width, P):
+                        k = (unit_tap + col) // P
+                        nc.tensor.matmul(total[:], flipped[:, HIT, col : col + P], w_sign["hit"][:, k, :],
+                                         start=(k == 0), stop=False)
+                        nc.tensor.matmul(total[:], flipped[:, MISS, col : col + P], w_sign["miss"][:, k, :],
+                                         start=False, stop=(k == K_TILES - 1))
+                piece_tap += width
             scaled = work.tile([P, F], F32, name="scaled")
             nc.scalar.mul(scaled[:], total[:], gamma_abs[:, 0:1])
             nc.sync.dma_start(out[b * P : (b + 1) * P, :], scaled[:])

@@ -12,10 +12,11 @@ C, S, F, R = 256, 1152, 128, 3
 BLOCKS = C // P
 K_TILES = S // P
 RUN_COLS = S // 16
-PIECES = ((512, 640), (640, 256, 128, 128))
+PIECES = ((512, 640), (512, 256, 256, 128))
 WIDEST = max(max(widths) for widths in PIECES)
 UNIT = 256
-X0_CUTS = 3
+PARTS = (3, 1)
+HIT, MISS = 0, 1
 
 FLOPS = 2 * 2 * C * S * F
 
@@ -25,54 +26,58 @@ def tile_binary_conv_kernel(tc, x, w_hit, w_miss, gamma, offs, out):
     with (
         tc.tile_pool(name="held", bufs=1) as held,
         tc.tile_pool(name="block", bufs=BLOCKS) as block,
-        tc.tile_pool(name="work", bufs=3) as work,
-        tc.psum_pool(name="flip", bufs=4) as flip,
+        tc.tile_pool(name="work", bufs=6) as work,
+        tc.psum_pool(name="flip", bufs=3) as flip,
         tc.psum_pool(name="sums", bufs=BLOCKS) as sums,
     ):
         offsets = held.tile([P, R * RUN_COLS], U16, name="offsets")
         nc.sync.dma_start(offsets[:], offs)
-        cuts = {0: X0_CUTS, 1: 1}
-        x_blocks = [block.tile([P, S], F32, name="x_sb") for b in range(BLOCKS)]
-        for j in range(X0_CUTS):
-            cols = slice(j * (S // X0_CUTS), (j + 1) * (S // X0_CUTS))
-            queue = nc.scalar if j % 2 == 0 else nc.sync
-            queue.dma_start(x_blocks[0][:, cols], x[0:P, cols])
-        w_raw = {}
-        for name, w, queue in (("hit", w_hit, nc.sync), ("miss", w_miss, nc.scalar)):
-            w_raw[name] = held.tile([P, K_TILES, F], F32, name="w_raw_" + name)
-            queue.dma_start(w_raw[name][:], w.rearrange("(k p) f -> p k f", p=P))
-        nc.sync.dma_start(x_blocks[1][:], x[P : 2 * P, :])
+        queues = (nc.scalar, nc.sync)
+        x_blocks = []
+        for b in range(BLOCKS):
+            x_sb = block.tile([P, S], F32, name="x_sb")
+            part = S // PARTS[b]
+            for j in range(PARTS[b]):
+                cols = slice(j * part, (j + 1) * part)
+                queues[j % 2].dma_start(x_sb[:, cols], x[b * P : (b + 1) * P, cols])
+            x_blocks.append(x_sb)
+        w_raw = []
+        for w, queue in zip((w_hit, w_miss), (nc.sync, nc.scalar)):
+            raw = held.tile([P, K_TILES, F], F32, name="w_raw" + str(len(w_raw)))
+            queue.dma_start(raw[:], w.rearrange("(k p) f -> p k f", p=P))
+            w_raw.append(raw)
         gamma_sb = held.tile([P, 1], F32, name="gamma_sb")
-        nc.scalar.dma_start(gamma_sb[:], gamma.partition_broadcast(P))
+        nc.sync.dma_start(gamma_sb[:], gamma.partition_broadcast(P))
 
         identity = held.tile([P, P], F32, name="identity")
         make_identity(nc, identity[:])
 
-        sel_blocks, minus_x_blocks = [], []
-        w_sign = {}
+        sel_blocks = []
+        minus_x_blocks = [block.tile([P, S], F32, name="minus_x") for b in range(BLOCKS)]
         for b in range(BLOCKS):
             x_sb = x_blocks[b]
             sgn = block.tile([P, S], F32, name="sgn")
             sel = block.tile([P, S], F32, name="sel")
-            for j in range(cuts[b]):
-                cols = slice(j * (S // cuts[b]), (j + 1) * (S // cuts[b]))
+            part = S // PARTS[b]
+            for j in range(PARTS[b]):
+                cols = slice(j * part, (j + 1) * part)
                 nc.scalar.activation(sgn[:, cols], x_sb[:, cols], ACT.Sign)
                 if b == 0:
                     nc.vector.tensor_scalar(sel[:, cols], sgn[:, cols], 0.5, 0.5, ALU.mult, ALU.add)
                 else:
                     nc.scalar.activation(sel[:, cols], sgn[:, cols], ACT.Copy, bias=0.5, scale=0.5)
-            minus_x = block.tile([P, S], F32, name="minus_x")
-            nc.scalar.mul(minus_x[:], x_sb[:], -1.0)
             sel_blocks.append(sel)
-            minus_x_blocks.append(minus_x)
             if b == 0:
-                for name in ("hit", "miss"):
-                    w_sign[name] = held.tile([P, K_TILES, F], BF16, name="w_sign_" + name)
-                    nc.scalar.activation(w_sign[name][:], w_raw[name][:], ACT.Sign)
-                gamma_abs = held.tile([P, 1], F32, name="gamma_abs")
-                nc.scalar.activation(gamma_abs[:], gamma_sb[:], ACT.Abs)
+                nc.scalar.mul(minus_x_blocks[0][:], x_sb[:], -1.0)
 
-        HIT, MISS = 0, 1
+        w_sign = []
+        for raw in w_raw:
+            binary = held.tile([P, K_TILES, F], BF16, name="w_sign" + str(len(w_sign)))
+            nc.scalar.activation(binary[:], raw[:], ACT.Sign)
+            w_sign.append(binary)
+        gamma_abs = held.tile([P, 1], F32, name="gamma_abs")
+        nc.scalar.activation(gamma_abs[:], gamma_sb[:], ACT.Abs)
+
         for b in range(BLOCKS):
             x_sb, sel, minus_x = x_blocks[b], sel_blocks[b], minus_x_blocks[b]
             total = sums.tile([P, F], F32, name="total")
@@ -102,10 +107,12 @@ def tile_binary_conv_kernel(tc, x, w_hit, w_miss, gamma, offs, out):
                     nc.scalar.activation(flipped[:], turned[:], ACT.Abs)
                     for col in range(0, unit_width, P):
                         k = (unit_tap + col) // P
-                        nc.tensor.matmul(total[:], flipped[:, HIT, col : col + P], w_sign["hit"][:, k, :],
-                                         start=(k == 0), stop=False)
-                        nc.tensor.matmul(total[:], flipped[:, MISS, col : col + P], w_sign["miss"][:, k, :],
-                                         start=False, stop=(k == K_TILES - 1))
+                        for kind in (HIT, MISS):
+                            nc.tensor.matmul(total[:], flipped[:, kind, col : col + P], w_sign[kind][:, k, :],
+                                             start=(k == 0 and kind == HIT),
+                                             stop=(k == K_TILES - 1 and kind == MISS))
+                if piece_tap == 0 and b + 1 < BLOCKS:
+                    nc.scalar.mul(minus_x_blocks[b + 1][:], x_blocks[b + 1][:], -1.0)
                 piece_tap += width
             scaled = work.tile([P, F], F32, name="scaled")
             nc.scalar.mul(scaled[:], total[:], gamma_abs[:, 0:1])

@@ -78,9 +78,23 @@ def tile_binary_conv_kernel(tc, x, w_hit, w_miss, gamma, offs, out):
         gamma_abs = held.tile([P, 1], F32, name="gamma_abs")
         nc.scalar.activation(gamma_abs[:], gamma_sb[:], ACT.Abs)
 
+        totals = [sums.tile([P, F], F32, name="total") for b in range(BLOCKS)]
+
+        def multiply(b, unit_tap, unit_width, flipped):
+            for col in range(0, unit_width, P):
+                k = (unit_tap + col) // P
+                for kind in (HIT, MISS):
+                    nc.tensor.matmul(totals[b][:], flipped[:, kind, col : col + P], w_sign[kind][:, k, :],
+                                     start=(k == 0 and kind == HIT),
+                                     stop=(k == K_TILES - 1 and kind == MISS))
+            if unit_tap + unit_width == S:
+                scaled = work.tile([P, F], F32, name="scaled")
+                nc.scalar.mul(scaled[:], totals[b][:], gamma_abs[:, 0:1])
+                nc.sync.dma_start(out[b * P : (b + 1) * P, :], scaled[:])
+
+        late = None
         for b in range(BLOCKS):
             x_sb, sel, minus_x = x_blocks[b], sel_blocks[b], minus_x_blocks[b]
-            total = sums.tile([P, F], F32, name="total")
             piece_tap = 0
             for width in PIECES[b]:
                 signed = x_sb[:, piece_tap : piece_tap + width]
@@ -105,15 +119,10 @@ def tile_binary_conv_kernel(tc, x, w_hit, w_miss, gamma, offs, out):
                         nc.tensor.transpose(turned[:, HIT, col : col + P], rows, identity[:])
                     flipped = work.tile([P, 2, unit_width], BF16, name="flipped")
                     nc.scalar.activation(flipped[:], turned[:], ACT.Abs)
-                    for col in range(0, unit_width, P):
-                        k = (unit_tap + col) // P
-                        for kind in (HIT, MISS):
-                            nc.tensor.matmul(total[:], flipped[:, kind, col : col + P], w_sign[kind][:, k, :],
-                                             start=(k == 0 and kind == HIT),
-                                             stop=(k == K_TILES - 1 and kind == MISS))
+                    if late is not None:
+                        multiply(*late)
+                    late = (b, unit_tap, unit_width, flipped)
                 if piece_tap == 0 and b + 1 < BLOCKS:
                     nc.scalar.mul(minus_x_blocks[b + 1][:], x_blocks[b + 1][:], -1.0)
                 piece_tap += width
-            scaled = work.tile([P, F], F32, name="scaled")
-            nc.scalar.mul(scaled[:], total[:], gamma_abs[:, 0:1])
-            nc.sync.dma_start(out[b * P : (b + 1) * P, :], scaled[:])
+        multiply(*late)

@@ -84,7 +84,7 @@ def tile_binary_conv_kernel(tc, x, w_hit, w_miss, gamma, offs, out):
             for col in range(0, unit_width, P):
                 k = (unit_tap + col) // P
                 for kind in (HIT, MISS):
-                    nc.tensor.matmul(totals[b][:], flipped[:, kind, col : col + P], w_sign[kind][:, k, :],
+                    nc.tensor.matmul(totals[b][:], flipped[kind][:, col : col + P], w_sign[kind][:, k, :],
                                      start=(k == 0 and kind == HIT),
                                      stop=(k == K_TILES - 1 and kind == MISS))
             if unit_tap + unit_width == S:
@@ -108,17 +108,23 @@ def tile_binary_conv_kernel(tc, x, w_hit, w_miss, gamma, offs, out):
                 for unit_col in range(0, width, UNIT):
                     unit_width = min(UNIT, width - unit_col)
                     unit_tap = piece_tap + unit_col
-                    turned = flip.tile([P, 2, unit_width], F32, name="turned")
+                    turned_hit = flip.tile([P, unit_width], F32, name="turned_hit")
                     for col in range(0, unit_width, P):
-                        rows = signed[:, unit_col + col : unit_col + col + P]
-                        nc.tensor.matmul(turned[:, MISS, col : col + P],
+                        nc.tensor.transpose(turned_hit[:, col : col + P],
+                                            signed[:, unit_col + col : unit_col + col + P], identity[:])
+                    flipped_hit = work.tile([P, unit_width], BF16, name="flipped_hit")
+                    nc.scalar.activation(flipped_hit[:], turned_hit[:], ACT.Abs)
+                    turned_miss = flip.tile([P, unit_width], F32, name="turned_miss")
+                    for col in range(0, unit_width, P):
+                        nc.tensor.matmul(turned_miss[:, col : col + P],
                                          minus_x[:, unit_tap + col : unit_tap + col + P], identity[:],
                                          is_transpose=True, start=True, stop=False)
-                        nc.tensor.matmul(turned[:, MISS, col : col + P], rows, identity[:],
+                        nc.tensor.matmul(turned_miss[:, col : col + P],
+                                         signed[:, unit_col + col : unit_col + col + P], identity[:],
                                          is_transpose=True, start=False, stop=True)
-                        nc.tensor.transpose(turned[:, HIT, col : col + P], rows, identity[:])
-                    flipped = work.tile([P, 2, unit_width], BF16, name="flipped")
-                    nc.scalar.activation(flipped[:], turned[:], ACT.Abs)
+                    flipped_miss = work.tile([P, unit_width], BF16, name="flipped_miss")
+                    nc.scalar.activation(flipped_miss[:], turned_miss[:], ACT.Abs)
+                    flipped = (flipped_hit, flipped_miss)
                     if late is not None:
                         multiply(*late)
                     late = (b, unit_tap, unit_width, flipped)

@@ -15,7 +15,7 @@ RUN_COLS = S // 16
 PIECES = ((512, 640), (512, 256, 256, 128))
 WIDEST = max(max(widths) for widths in PIECES)
 UNIT = 256
-PARTS = (3, 1)
+PARTS = ((128, 384, 384, 256), (S,))
 HIT, MISS = 0, 1
 
 FLOPS = 2 * 2 * C * S * F
@@ -32,19 +32,17 @@ def tile_binary_conv_kernel(tc, x, w_hit, w_miss, gamma, offs, out):
     ):
         offsets = held.tile([P, R * RUN_COLS], U16, name="offsets")
         nc.sync.dma_start(offsets[:], offs)
-        queues = (nc.scalar, nc.sync)
         x_blocks = []
         for b in range(BLOCKS):
             x_sb = block.tile([P, S], F32, name="x_sb")
-            part = S // PARTS[b]
-            for j in range(PARTS[b]):
-                cols = slice(j * part, (j + 1) * part)
-                queues[j % 2].dma_start(x_sb[:, cols], x[b * P : (b + 1) * P, cols])
+            for j, part in enumerate(PARTS[b]):
+                cols = slice(sum(PARTS[b][:j]), sum(PARTS[b][:j]) + part)
+                nc.sync.dma_start(x_sb[:, cols], x[b * P : (b + 1) * P, cols])
             x_blocks.append(x_sb)
         w_raw = []
-        for w, queue in zip((w_hit, w_miss), (nc.sync, nc.scalar)):
+        for w in (w_hit, w_miss):
             raw = held.tile([P, K_TILES, F], F32, name="w_raw" + str(len(w_raw)))
-            queue.dma_start(raw[:], w.rearrange("(k p) f -> p k f", p=P))
+            nc.sync.dma_start(raw[:], w.rearrange("(k p) f -> p k f", p=P))
             w_raw.append(raw)
         gamma_sb = held.tile([P, 1], F32, name="gamma_sb")
         nc.sync.dma_start(gamma_sb[:], gamma.partition_broadcast(P))
@@ -58,9 +56,8 @@ def tile_binary_conv_kernel(tc, x, w_hit, w_miss, gamma, offs, out):
             x_sb = x_blocks[b]
             sgn = block.tile([P, S], F32, name="sgn")
             sel = block.tile([P, S], F32, name="sel")
-            part = S // PARTS[b]
-            for j in range(PARTS[b]):
-                cols = slice(j * part, (j + 1) * part)
+            for j, part in enumerate(PARTS[b]):
+                cols = slice(sum(PARTS[b][:j]), sum(PARTS[b][:j]) + part)
                 nc.scalar.activation(sgn[:, cols], x_sb[:, cols], ACT.Sign)
                 if b == 0:
                     nc.vector.tensor_scalar(sel[:, cols], sgn[:, cols], 0.5, 0.5, ALU.mult, ALU.add)

@@ -31,7 +31,6 @@ def tile_binary_conv_kernel(tc, x, w_hit, w_miss, gamma, offs, out):
         tc.psum_pool(name="sums", bufs=BLOCKS) as sums,
     ):
         offsets = held.tile([P, R * RUN_COLS], U16, name="offsets")
-        nc.sync.dma_start(offsets[:], offs)
         x_blocks = []
         for b in range(BLOCKS):
             x_sb = block.tile([P, S], F32, name="x_sb")
@@ -39,6 +38,8 @@ def tile_binary_conv_kernel(tc, x, w_hit, w_miss, gamma, offs, out):
                 cols = slice(sum(PARTS[b][:j]), sum(PARTS[b][:j]) + part)
                 nc.sync.dma_start(x_sb[:, cols], x[b * P : (b + 1) * P, cols])
             x_blocks.append(x_sb)
+            if b == 0:
+                nc.sync.dma_start(offsets[:], offs)
         w_raw = []
         for w in (w_hit, w_miss):
             raw = held.tile([P, K_TILES, F], F32, name="w_raw" + str(len(w_raw)))

@@ -15,7 +15,7 @@ RUN_COLS = S // 16
 PIECES = ((512, 640), (512, 256, 256, 128))
 WIDEST = max(max(widths) for widths in PIECES)
 UNIT = 256
-PARTS = ((128, 384, 384, 256), (S,))
+PARTS = ((384, 384, 256, 128), (S,))
 HIT, MISS = 0, 1
 
 FLOPS = 2 * 2 * C * S * F

@@ -88,7 +88,7 @@ def tile_binary_conv_kernel(tc, x, w_hit, w_miss, gamma, offs, out):
             if unit_tap + unit_width == S:
                 scaled = work.tile([P, F], F32, name="scaled")
                 nc.scalar.mul(scaled[:], totals[b][:], gamma_abs[:, 0:1])
-                nc.sync.dma_start(out[b * P : (b + 1) * P, :], scaled[:])
+                nc.scalar.dma_start(out[b * P : (b + 1) * P, :], scaled[:])
 
         late = None
         for b in range(BLOCKS):

@@ -81,10 +81,10 @@ def tile_binary_conv_kernel(tc, x, w_hit, w_miss, gamma, offs, out):
         def multiply(b, unit_tap, unit_width, flipped):
             for col in range(0, unit_width, P):
                 k = (unit_tap + col) // P
-                for kind in (HIT, MISS):
+                for kind in (MISS, HIT):
                     nc.tensor.matmul(totals[b][:], flipped[kind][:, col : col + P], w_sign[kind][:, k, :],
-                                     start=(k == 0 and kind == HIT),
-                                     stop=(k == K_TILES - 1 and kind == MISS))
+                                     start=(k == 0 and kind == MISS),
+                                     stop=(k == K_TILES - 1 and kind == HIT))
             if unit_tap + unit_width == S:
                 scaled = work.tile([P, F], F32, name="scaled")
                 nc.scalar.mul(scaled[:], totals[b][:], gamma_abs[:, 0:1])
@@ -106,12 +106,6 @@ def tile_binary_conv_kernel(tc, x, w_hit, w_miss, gamma, offs, out):
                 for unit_col in range(0, width, UNIT):
                     unit_width = min(UNIT, width - unit_col)
                     unit_tap = piece_tap + unit_col
-                    turned_hit = flip.tile([P, unit_width], F32, name="turned_hit")
-                    for col in range(0, unit_width, P):
-                        nc.tensor.transpose(turned_hit[:, col : col + P],
-                                            signed[:, unit_col + col : unit_col + col + P], identity[:])
-                    flipped_hit = work.tile([P, unit_width], BF16, name="flipped_hit")
-                    nc.scalar.activation(flipped_hit[:], turned_hit[:], ACT.Abs)
                     turned_miss = flip.tile([P, unit_width], F32, name="turned_miss")
                     for col in range(0, unit_width, P):
                         nc.tensor.matmul(turned_miss[:, col : col + P],
@@ -122,6 +116,12 @@ def tile_binary_conv_kernel(tc, x, w_hit, w_miss, gamma, offs, out):
                                          is_transpose=True, start=False, stop=True)
                     flipped_miss = work.tile([P, unit_width], BF16, name="flipped_miss")
                     nc.scalar.activation(flipped_miss[:], turned_miss[:], ACT.Abs)
+                    turned_hit = flip.tile([P, unit_width], F32, name="turned_hit")
+                    for col in range(0, unit_width, P):
+                        nc.tensor.transpose(turned_hit[:, col : col + P],
+                                            signed[:, unit_col + col : unit_col + col + P], identity[:])
+                    flipped_hit = work.tile([P, unit_width], BF16, name="flipped_hit")
+                    nc.scalar.activation(flipped_hit[:], turned_hit[:], ACT.Abs)
                     flipped = (flipped_hit, flipped_miss)
                     if late is not None:
                         multiply(*late)

@@ -15,7 +15,8 @@ RUN_COLS = S // 16
 PIECES = ((512, 640), (512, 256, 256, 128))
 WIDEST = max(max(widths) for widths in PIECES)
 UNIT = 256
-PARTS = ((384, 384, 256, 128), (S,))
+PARTS = ((256, 256, 256, 256, 128), (S,))
+VECTORS_PART = 1
 HIT, MISS = 0, 1
 
 FLOPS = 2 * 2 * C * S * F
@@ -59,6 +60,12 @@ def tile_binary_conv_kernel(tc, x, w_hit, w_miss, gamma, offs, out):
             sel = block.tile([P, S], F32, name="sel")
             for j, part in enumerate(PARTS[b]):
                 cols = slice(sum(PARTS[b][:j]), sum(PARTS[b][:j]) + part)
+                if b == 0 and j == VECTORS_PART:
+                    half_or_one = held.tile([P, part], F32, name="half_or_one")
+                    nc.vector.tensor_scalar(half_or_one[:], x_sb[:, cols], 0.0, 0.5, ALU.is_gt, ALU.max)
+                    nc.vector.scalar_tensor_tensor(sel[:, cols], x_sb[:, cols], 0.0, half_or_one[:],
+                                                   ALU.is_ge, ALU.mult)
+                    continue
                 nc.scalar.activation(sgn[:, cols], x_sb[:, cols], ACT.Sign)
                 if b == 0:
                     nc.vector.tensor_scalar(sel[:, cols], sgn[:, cols], 0.5, 0.5, ALU.mult, ALU.add)

@@ -14,7 +14,7 @@ K_TILES = S // P
 RUN_COLS = S // 16
 PIECES = ((512, 640), (512, 256, 256, 128))
 WIDEST = max(max(widths) for widths in PIECES)
-UNIT = 256
+UNIT = 512
 PARTS = ((256, 256, 256, 256, 128), (S,))
 VECTORS_PART = 1
 HIT, MISS = 0, 1
@@ -72,8 +72,7 @@ def tile_binary_conv_kernel(tc, x, w_hit, w_miss, gamma, offs, out):
                 else:
                     nc.scalar.activation(sel[:, cols], sgn[:, cols], ACT.Copy, bias=0.5, scale=0.5)
             sel_blocks.append(sel)
-            if b == 0:
-                nc.scalar.mul(minus_x_blocks[0][:], x_sb[:], -1.0)
+            nc.scalar.mul(minus_x_blocks[b][:], x_sb[:], -1.0)
 
         w_sign = []
         for raw in w_raw:
@@ -84,6 +83,46 @@ def tile_binary_conv_kernel(tc, x, w_hit, w_miss, gamma, offs, out):
         nc.scalar.activation(gamma_abs[:], gamma_sb[:], ACT.Abs)
 
         totals = [sums.tile([P, F], F32, name="total") for b in range(BLOCKS)]
+        pieces = [(b, sum(PIECES[b][:i]), width) for b in range(BLOCKS) for i, width in enumerate(PIECES[b])]
+
+        def units_of(piece_tap, width):
+            return [(piece_tap + col, min(UNIT, width - col)) for col in range(0, width, UNIT)]
+
+        def begin_miss(b, piece_tap, width):
+            begun = []
+            for unit_tap, unit_width in units_of(piece_tap, width):
+                turned_miss = flip.tile([P, unit_width], F32, name="turned_miss")
+                for col in range(0, unit_width, P):
+                    nc.tensor.matmul(turned_miss[:, col : col + P],
+                                     minus_x_blocks[b][:, unit_tap + col : unit_tap + col + P], identity[:],
+                                     is_transpose=True, start=(col == 0), stop=False)
+                begun.append(turned_miss)
+            return begun
+
+        def look_up(b, piece_tap, width):
+            signed = x_blocks[b][:, piece_tap : piece_tap + width]
+            for r in range(R):
+                first = r * RUN_COLS + piece_tap // 16
+                picked = sel_blocks[b][:].indirect(offsets[:, first : first + width // 16])
+                longer = work.tile([P, WIDEST], F32, name="product" + str(r))
+                nc.vector.tensor_tensor(longer[:, :width], picked, signed, ALU.mult)
+                signed = longer[:, :width]
+            return signed
+
+        def flip_unit(piece_tap, unit_tap, unit_width, signed, turned_miss):
+            for col in range(0, unit_width, P):
+                at = unit_tap - piece_tap + col
+                nc.tensor.matmul(turned_miss[:, col : col + P], signed[:, at : at + P], identity[:],
+                                 is_transpose=True, start=False, stop=(col + P == unit_width))
+            flipped_miss = work.tile([P, unit_width], BF16, name="flipped_miss")
+            nc.scalar.activation(flipped_miss[:], turned_miss[:], ACT.Abs)
+            turned_hit = flip.tile([P, unit_width], F32, name="turned_hit")
+            for col in range(0, unit_width, P):
+                at = unit_tap - piece_tap + col
+                nc.tensor.transpose(turned_hit[:, col : col + P], signed[:, at : at + P], identity[:])
+            flipped_hit = work.tile([P, unit_width], BF16, name="flipped_hit")
+            nc.scalar.activation(flipped_hit[:], turned_hit[:], ACT.Abs)
+            return (flipped_hit, flipped_miss)
 
         def multiply(b, unit_tap, unit_width, flipped):
             for col in range(0, unit_width, P):
@@ -97,43 +136,17 @@ def tile_binary_conv_kernel(tc, x, w_hit, w_miss, gamma, offs, out):
                 nc.scalar.mul(scaled[:], totals[b][:], gamma_abs[:, 0:1])
                 nc.scalar.dma_start(out[b * P : (b + 1) * P, :], scaled[:])
 
+        begun, products = [], []
         late = None
-        for b in range(BLOCKS):
-            x_sb, sel, minus_x = x_blocks[b], sel_blocks[b], minus_x_blocks[b]
-            piece_tap = 0
-            for width in PIECES[b]:
-                signed = x_sb[:, piece_tap : piece_tap + width]
-                for r in range(R):
-                    first = r * RUN_COLS + piece_tap // 16
-                    picked = sel[:].indirect(offsets[:, first : first + width // 16])
-                    longer = work.tile([P, WIDEST], F32, name="product" + str(r))
-                    nc.vector.tensor_tensor(longer[:, :width], picked, signed, ALU.mult)
-                    signed = longer[:, :width]
-
-                for unit_col in range(0, width, UNIT):
-                    unit_width = min(UNIT, width - unit_col)
-                    unit_tap = piece_tap + unit_col
-                    turned_miss = flip.tile([P, unit_width], F32, name="turned_miss")
-                    for col in range(0, unit_width, P):
-                        nc.tensor.matmul(turned_miss[:, col : col + P],
-                                         minus_x[:, unit_tap + col : unit_tap + col + P], identity[:],
-                                         is_transpose=True, start=True, stop=False)
-                        nc.tensor.matmul(turned_miss[:, col : col + P],
-                                         signed[:, unit_col + col : unit_col + col + P], identity[:],
-                                         is_transpose=True, start=False, stop=True)
-                    flipped_miss = work.tile([P, unit_width], BF16, name="flipped_miss")
-                    nc.scalar.activation(flipped_miss[:], turned_miss[:], ACT.Abs)
-                    turned_hit = flip.tile([P, unit_width], F32, name="turned_hit")
-                    for col in range(0, unit_width, P):
-                        nc.tensor.transpose(turned_hit[:, col : col + P],
-                                            signed[:, unit_col + col : unit_col + col + P], identity[:])
-                    flipped_hit = work.tile([P, unit_width], BF16, name="flipped_hit")
-                    nc.scalar.activation(flipped_hit[:], turned_hit[:], ACT.Abs)
-                    flipped = (flipped_hit, flipped_miss)
+        for i in range(len(pieces) + 1):
+            if i < len(pieces):
+                begun.append(begin_miss(*pieces[i]))
+                products.append(look_up(*pieces[i]))
+            if i > 0:
+                b, piece_tap, width = pieces[i - 1]
+                for unit, turned_miss in zip(units_of(piece_tap, width), begun[i - 1]):
+                    flipped = flip_unit(piece_tap, unit[0], unit[1], products[i - 1], turned_miss)
                     if late is not None:
                         multiply(*late)
-                    late = (b, unit_tap, unit_width, flipped)
-                if piece_tap == 0 and b + 1 < BLOCKS:
-                    nc.scalar.mul(minus_x_blocks[b + 1][:], x_blocks[b + 1][:], -1.0)
-                piece_tap += width
+                    late = (b, unit[0], unit[1], flipped)
         multiply(*late)

@@ -18,6 +18,7 @@ UNIT = 512
 PARTS = ((256, 256, 256, 256, 128), (S,))
 VECTORS_PART = 1
 HIT, MISS = 0, 1
+TAIL = PIECES[-1][-1]
 
 FLOPS = 2 * 2 * C * S * F
 
@@ -73,6 +74,9 @@ def tile_binary_conv_kernel(tc, x, w_hit, w_miss, gamma, offs, out):
                     nc.scalar.activation(sel[:, cols], sgn[:, cols], ACT.Copy, bias=0.5, scale=0.5)
             sel_blocks.append(sel)
             nc.scalar.mul(minus_x_blocks[b][:], x_sb[:], -1.0)
+        abs_tail = held.tile([P, TAIL], F32, name="abs_tail")
+        nc.scalar.activation(abs_tail[:], x_blocks[-1][:, S - TAIL :], ACT.Abs)
+        nc.scalar.mul(minus_x_blocks[-1][:, S - TAIL :], abs_tail[:], -1.0)
 
         w_sign = []
         for raw in w_raw:
@@ -100,7 +104,8 @@ def tile_binary_conv_kernel(tc, x, w_hit, w_miss, gamma, offs, out):
             return begun
 
         def look_up(b, piece_tap, width):
-            signed = x_blocks[b][:, piece_tap : piece_tap + width]
+            last_piece = b == BLOCKS - 1 and piece_tap == S - TAIL
+            signed = abs_tail[:] if last_piece else x_blocks[b][:, piece_tap : piece_tap + width]
             for r in range(R):
                 first = r * RUN_COLS + piece_tap // 16
                 picked = sel_blocks[b][:].indirect(offsets[:, first : first + width // 16])
@@ -109,7 +114,7 @@ def tile_binary_conv_kernel(tc, x, w_hit, w_miss, gamma, offs, out):
                 signed = longer[:, :width]
             return signed
 
-        def flip_unit(piece_tap, unit_tap, unit_width, signed, turned_miss):
+        def flip_unit(piece_tap, unit_tap, unit_width, signed, turned_miss, by_vector):
             for col in range(0, unit_width, P):
                 at = unit_tap - piece_tap + col
                 nc.tensor.matmul(turned_miss[:, col : col + P], signed[:, at : at + P], identity[:],
@@ -121,7 +126,10 @@ def tile_binary_conv_kernel(tc, x, w_hit, w_miss, gamma, offs, out):
                 at = unit_tap - piece_tap + col
                 nc.tensor.transpose(turned_hit[:, col : col + P], signed[:, at : at + P], identity[:])
             flipped_hit = work.tile([P, unit_width], BF16, name="flipped_hit")
-            nc.scalar.activation(flipped_hit[:], turned_hit[:], ACT.Abs)
+            if by_vector:
+                nc.vector.tensor_copy(flipped_hit[:], turned_hit[:])
+            else:
+                nc.scalar.activation(flipped_hit[:], turned_hit[:], ACT.Abs)
             return (flipped_hit, flipped_miss)
 
         def multiply(b, unit_tap, unit_width, flipped):
@@ -145,7 +153,7 @@ def tile_binary_conv_kernel(tc, x, w_hit, w_miss, gamma, offs, out):
             if i > 0:
                 b, piece_tap, width = pieces[i - 1]
                 for unit, turned_miss in zip(units_of(piece_tap, width), begun[i - 1]):
-                    flipped = flip_unit(piece_tap, unit[0], unit[1], products[i - 1], turned_miss)
+                    flipped = flip_unit(piece_tap, unit[0], unit[1], products[i - 1], turned_miss, i == len(pieces))
                     if late is not None:
                         multiply(*late)
                     late = (b, unit[0], unit[1], flipped)

import concourse.mybir as mybir
from concourse.masks import make_identity

F32 = mybir.dt.float32
BF16 = mybir.dt.bfloat16
U16 = mybir.dt.uint16
ACT = mybir.ActivationFunctionType
ALU = mybir.AluOpType

P = 128
C, S, F, R = 256, 1152, 128, 3
BLOCKS = C // P
K_TILES = S // P
RUN_COLS = S // 16
PIECES = ((512, 640), (512, 256, 256, 128))
WIDEST = max(max(widths) for widths in PIECES)
UNIT = 512
PARTS = ((256, 256, 256, 256, 128), (S,))
VECTORS_PART = 1
HIT, MISS = 0, 1
TAIL = PIECES[-1][-1]

FLOPS = 2 * 2 * C * S * F


def tile_binary_conv_kernel(tc, x, w_hit, w_miss, gamma, offs, out):
    nc = tc.nc
    with (
        tc.tile_pool(name="held", bufs=1) as held,
        tc.tile_pool(name="block", bufs=BLOCKS) as block,
        tc.tile_pool(name="work", bufs=6) as work,
        tc.psum_pool(name="flip", bufs=3) as flip,
        tc.psum_pool(name="sums", bufs=BLOCKS) as sums,
    ):
        offsets = held.tile([P, R * RUN_COLS], U16, name="offsets")
        x_blocks = []
        for b in range(BLOCKS):
            x_sb = block.tile([P, S], F32, name="x_sb")
            for j, part in enumerate(PARTS[b]):
                cols = slice(sum(PARTS[b][:j]), sum(PARTS[b][:j]) + part)
                nc.sync.dma_start(x_sb[:, cols], x[b * P : (b + 1) * P, cols])
            x_blocks.append(x_sb)
            if b == 0:
                nc.sync.dma_start(offsets[:], offs)
        w_raw = []
        for w in (w_hit, w_miss):
            raw = held.tile([P, K_TILES, F], F32, name="w_raw" + str(len(w_raw)))
            nc.sync.dma_start(raw[:], w.rearrange("(k p) f -> p k f", p=P))
            w_raw.append(raw)
        gamma_sb = held.tile([P, 1], F32, name="gamma_sb")
        nc.sync.dma_start(gamma_sb[:], gamma.partition_broadcast(P))

        identity = held.tile([P, P], F32, name="identity")
        make_identity(nc, identity[:])

        sel_blocks = []
        minus_x_blocks = [block.tile([P, S], F32, name="minus_x") for b in range(BLOCKS)]
        for b in range(BLOCKS):
            x_sb = x_blocks[b]
            sgn = block.tile([P, S], F32, name="sgn")
            sel = block.tile([P, S], F32, name="sel")
            for j, part in enumerate(PARTS[b]):
                cols = slice(sum(PARTS[b][:j]), sum(PARTS[b][:j]) + part)
                if b == 0 and j == VECTORS_PART:
                    half_or_one = held.tile([P, part], F32, name="half_or_one")
                    nc.vector.tensor_scalar(half_or_one[:], x_sb[:, cols], 0.0, 0.5, ALU.is_gt, ALU.max)
                    nc.vector.scalar_tensor_tensor(sel[:, cols], x_sb[:, cols], 0.0, half_or_one[:],
                                                   ALU.is_ge, ALU.mult)
                    continue
                nc.scalar.activation(sgn[:, cols], x_sb[:, cols], ACT.Sign)
                if b == 0:
                    nc.vector.tensor_scalar(sel[:, cols], sgn[:, cols], 0.5, 0.5, ALU.mult, ALU.add)
                else:
                    nc.scalar.activation(sel[:, cols], sgn[:, cols], ACT.Copy, bias=0.5, scale=0.5)
            sel_blocks.append(sel)
            nc.scalar.mul(minus_x_blocks[b][:], x_sb[:], -1.0)
        abs_tail = held.tile([P, TAIL], F32, name="abs_tail")
        nc.scalar.activation(abs_tail[:], x_blocks[-1][:, S - TAIL :], ACT.Abs)
        nc.scalar.mul(minus_x_blocks[-1][:, S - TAIL :], abs_tail[:], -1.0)

        w_sign = []
        for raw in w_raw:
            binary = held.tile([P, K_TILES, F], BF16, name="w_sign" + str(len(w_sign)))
            nc.scalar.activation(binary[:], raw[:], ACT.Sign)
            w_sign.append(binary)
        gamma_abs = held.tile([P, 1], F32, name="gamma_abs")
        nc.scalar.activation(gamma_abs[:], gamma_sb[:], ACT.Abs)

        totals = [sums.tile([P, F], F32, name="total") for b in range(BLOCKS)]
        pieces = [(b, sum(PIECES[b][:i]), width) for b in range(BLOCKS) for i, width in enumerate(PIECES[b])]

        def units_of(piece_tap, width):
            return [(piece_tap + col, min(UNIT, width - col)) for col in range(0, width, UNIT)]

        def begin_miss(b, piece_tap, width):
            begun = []
            for unit_tap, unit_width in units_of(piece_tap, width):
                turned_miss = flip.tile([P, unit_width], F32, name="turned_miss")
                for col in range(0, unit_width, P):
                    nc.tensor.matmul(turned_miss[:, col : col + P],
                                     minus_x_blocks[b][:, unit_tap + col : unit_tap + col + P], identity[:],
                                     is_transpose=True, start=(col == 0), stop=False)
                begun.append(turned_miss)
            return begun

        def look_up(b, piece_tap, width):
            last_piece = b == BLOCKS - 1 and piece_tap == S - TAIL
            signed = abs_tail[:] if last_piece else x_blocks[b][:, piece_tap : piece_tap + width]
            for r in range(R):
                first = r * RUN_COLS + piece_tap // 16
                picked = sel_blocks[b][:].indirect(offsets[:, first : first + width // 16])
                longer = work.tile([P, WIDEST], F32, name="product" + str(r))
                nc.vector.tensor_tensor(longer[:, :width], picked, signed, ALU.mult)
                signed = longer[:, :width]
            return signed

        def flip_unit(piece_tap, unit_tap, unit_width, signed, turned_miss, by_vector):
            for col in range(0, unit_width, P):
                at = unit_tap - piece_tap + col
                nc.tensor.matmul(turned_miss[:, col : col + P], signed[:, at : at + P], identity[:],
                                 is_transpose=True, start=False, stop=(col + P == unit_width))
            flipped_miss = work.tile([P, unit_width], BF16, name="flipped_miss")
            nc.scalar.activation(flipped_miss[:], turned_miss[:], ACT.Abs)
            turned_hit = flip.tile([P, unit_width], F32, name="turned_hit")
            for col in range(0, unit_width, P):
                at = unit_tap - piece_tap + col
                nc.tensor.transpose(turned_hit[:, col : col + P], signed[:, at : at + P], identity[:])
            flipped_hit = work.tile([P, unit_width], BF16, name="flipped_hit")
            if by_vector:
                nc.vector.tensor_copy(flipped_hit[:], turned_hit[:])
            else:
                nc.scalar.activation(flipped_hit[:], turned_hit[:], ACT.Abs)
            return (flipped_hit, flipped_miss)

        def multiply(b, unit_tap, unit_width, flipped):
            for col in range(0, unit_width, P):
                k = (unit_tap + col) // P
                for kind in (MISS, HIT):
                    nc.tensor.matmul(totals[b][:], flipped[kind][:, col : col + P], w_sign[kind][:, k, :],
                                     start=(k == 0 and kind == MISS),
                                     stop=(k == K_TILES - 1 and kind == HIT))
            if unit_tap + unit_width == S:
                scaled = work.tile([P, F], F32, name="scaled")
                nc.scalar.mul(scaled[:], totals[b][:], gamma_abs[:, 0:1])
                nc.scalar.dma_start(out[b * P : (b + 1) * P, :], scaled[:])

        begun, products = [], []
        late = None
        for i in range(len(pieces) + 1):
            if i < len(pieces):
                begun.append(begin_miss(*pieces[i]))
                products.append(look_up(*pieces[i]))
            if i > 0:
                b, piece_tap, width = pieces[i - 1]
                for unit, turned_miss in zip(units_of(piece_tap, width), begun[i - 1]):
                    flipped = flip_unit(piece_tap, unit[0], unit[1], products[i - 1], turned_miss, i == len(pieces))
                    if late is not None:
                        multiply(*late)
                    late = (b, unit[0], unit[1], flipped)
        multiply(*late)
